import numpy as np
import ml_dtypes


def mxq(x, axis, fmt="e4m3"):
    dtype, down = {"e4m3": (ml_dtypes.float8_e4m3fn, 7), "e5m2": (ml_dtypes.float8_e5m2, 14)}[fmt]
    v = np.moveaxis(np.asarray(x, np.float32).astype(ml_dtypes.bfloat16).astype(np.float64), axis, -1)
    blocks = v.reshape(v.shape[:-1] + (-1, 32))
    amax = np.abs(blocks).max(-1, keepdims=True)
    byte = np.maximum(np.where(amax > 0, np.frexp(amax)[1] - 1 + 127, 0) - down, 1)
    scale = np.exp2(byte - 127.0)
    codes = (blocks / scale).astype(np.float32).astype(dtype).astype(np.float64)
    return np.moveaxis((codes * scale).reshape(v.shape), -1, axis)


WIDE = False


def mx_kscale(k):
    if not WIDE:
        return np.ones(k)
    levels = np.array([10, -10, 5, -5, 0])
    a = np.random.permutation(np.resize(levels, k // 512 * 4)).reshape(k // 512, 4)
    idx = np.arange(k)
    return np.exp2(a[idx // 512, idx % 128 // 32])


BF16 = ml_dtypes.bfloat16


def bf(x):
    return np.asarray(x, np.float32).astype(BF16)


def f64(x):
    return np.asarray(x).astype(np.float64)


E2M1 = np.array([0.0, 0.5, 1.0, 1.5, 2.0, 3.0, 4.0, 6.0, -0.0, -0.5, -1.0, -1.5, -2.0, -3.0, -4.0, -6.0])


def pack_weight(w, fmt):
    k, n = w.shape
    w = f64(bf(w)).reshape(k // 32, 32, n)
    amax = np.abs(w).max(1)
    if fmt == "e4m3":
        byte = np.frexp(amax)[1] - 1 + 127 - 7
    else:
        mant, ex = np.frexp(amax / 6.0)
        byte = np.where(mant > 0.5, ex, ex - 1) + 127
    byte = np.clip(np.where(amax > 0, byte, 1), 1, 254)
    scaled = (w * np.exp2(127.0 - byte)[:, None, :]).reshape(k, n).astype(np.float32)
    by_word = np.ascontiguousarray(scaled.reshape(k // 512, 128, 4, n).transpose(0, 1, 3, 2))
    if fmt == "e4m3":
        words = by_word.astype(ml_dtypes.float8_e4m3fn).view(np.uint8)
    else:
        c = by_word.astype(ml_dtypes.float4_e2m1fn).view(np.uint8) & 0xF
        words = c[..., 0::2] | (c[..., 1::2] << 4)
    return np.ascontiguousarray(words), np.ascontiguousarray(byte.astype(np.uint8).reshape(k // 512, 16, n))


def unpack_weight(words, scales, fmt):
    g, p, n, _ = words.shape
    if fmt == "e4m3":
        vals = np.ascontiguousarray(words).view(ml_dtypes.float8_e4m3fn).astype(np.float64)
    else:
        nib = np.empty((g, p, n, 4), np.uint8)
        nib[..., 0::2] = words & 0xF
        nib[..., 1::2] = words >> 4
        vals = E2M1[nib]
    vals = vals * np.repeat(np.exp2(scales.astype(np.float64) - 127.0), 8, axis=1)[..., None]
    return vals.transpose(0, 1, 3, 2).reshape(g * 512, n)

def pack4(w):
    words, scales = pack_weight(w, "e2m1")
    return words.reshape(words.shape[0], 128, -1), scales


def unpack4(words, scales):
    return unpack_weight(words.reshape(words.shape[0], 128, -1, 2), scales, "e2m1")


B, NB, NL, NG, NK = 256, 512, 1536, 500, 3
N2 = 2 * NB


def setup_inputs():
    s = mx_kscale(N2)
    r = s[:NB]
    Volt = bf(np.random.standard_normal((B, N2)) * s)
    y = np.random.standard_normal((NB, N2)) * 4.0 / np.sqrt(N2) / s[None, :] / r[:, None]
    yc = np.random.standard_normal((NB, N2)) * 4.0 / np.sqrt(N2) / s[None, :] / r[:, None]
    PQ_Loads = bf(np.random.standard_normal((B, N2)))
    PQ_Gens = bf(np.random.standard_normal((B, N2)))
    y_words, y_scales = pack4(np.ascontiguousarray(y.T))
    yc_words, yc_scales = pack4(np.ascontiguousarray(yc.T))
    return {'Volt': Volt,
            'Y_top_words': y_words,
            'Y_top_scales': y_scales,
            'Yconj_top_words': yc_words,
            'Yconj_top_scales': yc_scales,
            'PQ_Loads': PQ_Loads,
            'PQ_Gens': PQ_Gens}


def reference(Volt, Y_top_words, Y_top_scales, Yconj_top_words, Yconj_top_scales, PQ_Loads, PQ_Gens):
    V = f64(Volt)
    Vq = mxq(V, 1, 'e4m3')
    YV = Vq @ unpack4(Y_top_words, Y_top_scales)
    YcV = Vq @ unpack4(Yconj_top_words, Yconj_top_scales)
    out = np.sum(V[:, :NB] * YV, axis=1) + np.sum(V[:, :NB] * YcV, axis=1)
    pq = f64(PQ_Loads) - f64(PQ_Gens)
    return out + np.sum(pq[:, :NB], axis=1) + np.sum(pq[:, NB:], axis=1)

@@ -1,0 +1,142 @@
+from contextlib import ExitStack
+
+import concourse.mybir as mybir
+from concourse.masks import make_identity
+
+F32 = mybir.dt.float32
+BF16 = mybir.dt.bfloat16
+I32 = mybir.dt.int32
+U32 = mybir.dt.uint32
+U8 = mybir.dt.uint8
+FP8X4 = mybir.dt.float8_e4m3fn_x4
+FP4X4 = mybir.dt.float4_e2m1fn_x4
+MULT = mybir.AluOpType.mult
+ADD = mybir.AluOpType.add
+COPY = mybir.ActivationFunctionType.Copy
+
+P = 128
+B = 256
+K = 1024
+NB = 512
+PACK = 4
+K_PASS = P * PACK
+PASSES = K // K_PASS
+B_TILES = B // P
+WEIGHTS = 2
+QUADRANTS = 4
+WORDS_PER_PASS = K_PASS // 2
+
+FLOPS = 2 * B * K * NB * WEIGHTS
+
+
+def tile_kktloss_pc_s_kernel(
+    tc, Volt, Y_top_words, Y_top_scales, Yconj_top_words, Yconj_top_scales, PQ_Loads, PQ_Gens, out
+):
+    nc = tc.nc
+    weight_words = [Y_top_words, Yconj_top_words]
+    weight_scales = [Y_top_scales, Yconj_top_scales]
+
+    with ExitStack() as stack:
+        keep = stack.enter_context(tc.tile_pool(name="keep", bufs=1))
+        psum = stack.enter_context(tc.psum_pool(name="psum", bufs=1))
+
+        volt = keep.tile([P, B_TILES, K], BF16)
+        loads = keep.tile([P, B_TILES, K], BF16)
+        gens = keep.tile([P, B_TILES, K], BF16)
+        w_words = keep.tile([P, WEIGHTS, PASSES, 2 * NB], U8, align_bytes=64)
+        w_scales = keep.tile([P, WEIGHTS, PASSES, NB], U8, align_bytes=64)
+        v_codes = keep.tile([P, B_TILES, PASSES * P], U32, align_bytes=64)
+        v_scales = keep.tile([P, B_TILES, PASSES * P], U8, align_bytes=64)
+        ident = keep.tile([P, P], F32)
+        result_cols = keep.tile([P, P], F32)
+
+        nc.vector.memset(w_scales[:].bitcast(I32), 0)
+        nc.vector.memset(result_cols[:], 0.0)
+        make_identity(nc, ident[:])
+
+        for bt in range(B_TILES):
+            nc.sync.dma_start(out=volt[:, bt, :], in_=Volt[bt * P : (bt + 1) * P, :])
+        for w in range(WEIGHTS):
+            by_row = weight_scales[w].bitcast(I32).rearrange("g (q r) n -> r q g n", r=PACK)
+            for r in range(PACK):
+                nc.sync.dma_start(out=w_scales[r:P:32, w, :, :].bitcast(I32), in_=by_row[r])
+            nc.sync.dma_start(
+                out=w_words[:, w, :, :].bitcast(I32),
+                in_=weight_words[w].bitcast(I32).rearrange("g p n -> p g n"),
+            )
+        for bt in range(B_TILES):
+            nc.sync.dma_start(out=loads[:, bt, :], in_=PQ_Loads[bt * P : (bt + 1) * P, :])
+        for bt in range(B_TILES):
+            nc.sync.dma_start(out=gens[:, bt, :], in_=PQ_Gens[bt * P : (bt + 1) * P, :])
+
+        for bt in range(B_TILES):
+            volt_words = volt[:, bt, :].bitcast(F32)
+            flipped = psum.tile([P, PASSES, 2, P], F32, name="flipped%d" % bt)
+            for g in range(PASSES):
+                for u in range(2):
+                    first = g * WORDS_PER_PASS + u
+                    nc.tensor.transpose(
+                        flipped[:, g, u, :],
+                        volt_words[:, first : (g + 1) * WORDS_PER_PASS : 2],
+                        ident[:],
+                    )
+            grouped = keep.tile([P, PASSES, P, PACK], BF16, align_bytes=64, name="grouped%d" % bt)
+            copy_out = nc.vector.tensor_copy if bt % 2 == 0 else nc.scalar.copy
+            copy_out(out=grouped[:].bitcast(F32), in_=flipped[:].rearrange("p g u b -> p g b u"))
+            nc.vector.quantize_mx(
+                out=v_codes[:, bt, :].bitcast(FP8X4),
+                scales=v_scales[:, bt, :],
+                in_=grouped[:].rearrange("p g b t -> p (g b t)"),
+            )
+
+        load_sum = keep.tile([P, B_TILES], F32)
+        gen_sum = keep.tile([P, B_TILES], F32)
+        load_copy = keep.tile([P, B_TILES, K], BF16)
+        gen_copy = keep.tile([P, B_TILES, K], BF16)
+        for bt in range(B_TILES):
+            nc.scalar.activation(
+                out=load_copy[:, bt, :], in_=loads[:, bt, :], func=COPY, accum_out=load_sum[:, bt : bt + 1]
+            )
+            nc.vector.tensor_scalar(
+                out=gen_copy[:, bt, :],
+                in0=gens[:, bt, :],
+                scalar1=1.0,
+                scalar2=None,
+                op0=MULT,
+                op1=ADD,
+                accum_out=gen_sum[:, bt : bt + 1],
+            )
+        net_load = keep.tile([P, B_TILES], F32)
+        nc.vector.tensor_sub(out=net_load[:], in0=load_sum[:], in1=gen_sum[:])
+
+        power = keep.tile([P, B_TILES], F32)
+        products = keep.tile([P, B_TILES, NB], F32)
+        for bt in range(B_TILES):
+            acc = psum.tile([P, NB], F32, name="acc%d" % bt)
+            for w in range(WEIGHTS):
+                for g in range(PASSES):
+                    nc.tensor.matmul_mx(
+                        out=acc[:],
+                        lhsT=v_codes[:, bt, g * P : (g + 1) * P].bitcast(FP8X4),
+                        lhsT_scale=v_scales[:, bt, g * P : (g + 1) * P],
+                        rhs=w_words[:, w, g, :].bitcast(FP4X4),
+                        rhs_scale=w_scales[:, w, g, :],
+                        start=(w == 0 and g == 0),
+                        stop=(w == WEIGHTS - 1 and g == PASSES - 1),
+                    )
+            nc.vector.scalar_tensor_tensor(
+                out=products[:, bt, :],
+                in0=acc[:],
+                scalar=1.0,
+                in1=volt[:, bt, 0:NB],
+                op0=MULT,
+                op1=MULT,
+                accum_out=power[:, bt : bt + 1],
+            )
+
+        nc.vector.tensor_add(out=result_cols[:, 0:B_TILES], in0=power[:], in1=net_load[:])
+        result_rows_ps = psum.tile([P, P], F32)
+        nc.tensor.transpose(result_rows_ps[:], result_cols[:], ident[:])
+        result_rows = keep.tile([P, P], F32)
+        nc.vector.tensor_copy(out=result_rows[0:B_TILES, :], in_=result_rows_ps[0:B_TILES, :])
+        nc.sync.dma_start(out=out.rearrange("(t p) -> t p", p=P), in_=result_rows[0:B_TILES, :])

@@ -12,6 +12,7 @@ FP8X4 = mybir.dt.float8_e4m3fn_x4
 FP4X4 = mybir.dt.float4_e2m1fn_x4
 MULT = mybir.AluOpType.mult
 ADD = mybir.AluOpType.add
+SUBTRACT = mybir.AluOpType.subtract
 COPY = mybir.ActivationFunctionType.Copy
 
 P = 128
@@ -23,7 +24,6 @@ K_PASS = P * PACK
 PASSES = K // K_PASS
 B_TILES = B // P
 WEIGHTS = 2
-QUADRANTS = 4
 WORDS_PER_PASS = K_PASS // 2
 
 FLOPS = 2 * B * K * NB * WEIGHTS
@@ -39,6 +39,7 @@ def tile_kktloss_pc_s_kernel(
     with ExitStack() as stack:
         keep = stack.enter_context(tc.tile_pool(name="keep", bufs=1))
         psum = stack.enter_context(tc.psum_pool(name="psum", bufs=1))
+        stack.enter_context(tc.manual_schedule())
 
         volt = keep.tile([P, B_TILES, K], BF16)
         loads = keep.tile([P, B_TILES, K], BF16)
@@ -54,20 +55,23 @@ def tile_kktloss_pc_s_kernel(
         nc.vector.memset(result_cols[:], 0.0)
         make_identity(nc, ident[:])
 
-        for bt in range(B_TILES):
-            nc.sync.dma_start(out=volt[:, bt, :], in_=Volt[bt * P : (bt + 1) * P, :])
-        for w in range(WEIGHTS):
+        def load_scale_rows(w):
             by_row = weight_scales[w].bitcast(I32).rearrange("g (q r) n -> r q g n", r=PACK)
             for r in range(PACK):
                 nc.sync.dma_start(out=w_scales[r:P:32, w, :, :].bitcast(I32), in_=by_row[r])
+
+        for bt in range(B_TILES):
+            nc.sync.dma_start(out=volt[:, bt, :], in_=Volt[bt * P : (bt + 1) * P, :])
+        load_scale_rows(0)
+        for w in range(WEIGHTS):
             nc.sync.dma_start(
                 out=w_words[:, w, :, :].bitcast(I32),
                 in_=weight_words[w].bitcast(I32).rearrange("g p n -> p g n"),
             )
+        load_scale_rows(1)
         for bt in range(B_TILES):
-            nc.sync.dma_start(out=loads[:, bt, :], in_=PQ_Loads[bt * P : (bt + 1) * P, :])
-        for bt in range(B_TILES):
-            nc.sync.dma_start(out=gens[:, bt, :], in_=PQ_Gens[bt * P : (bt + 1) * P, :])
+            nc.gpsimd.dma_start(out=loads[:, bt, :], in_=PQ_Loads[bt * P : (bt + 1) * P, :])
+            nc.gpsimd.dma_start(out=gens[:, bt, :], in_=PQ_Gens[bt * P : (bt + 1) * P, :])
 
         for bt in range(B_TILES):
             volt_words = volt[:, bt, :].bitcast(F32)
@@ -81,8 +85,7 @@ def tile_kktloss_pc_s_kernel(
                         ident[:],
                     )
             grouped = keep.tile([P, PASSES, P, PACK], BF16, align_bytes=64, name="grouped%d" % bt)
-            copy_out = nc.vector.tensor_copy if bt % 2 == 0 else nc.scalar.copy
-            copy_out(out=grouped[:].bitcast(F32), in_=flipped[:].rearrange("p g u b -> p g b u"))
+            nc.scalar.copy(out=grouped[:].bitcast(F32), in_=flipped[:].rearrange("p g u b -> p g b u"))
             nc.vector.quantize_mx(
                 out=v_codes[:, bt, :].bitcast(FP8X4),
                 scales=v_scales[:, bt, :],
@@ -91,12 +94,13 @@ def tile_kktloss_pc_s_kernel(
 
         load_sum = keep.tile([P, B_TILES], F32)
         gen_sum = keep.tile([P, B_TILES], F32)
+        power = keep.tile([P, B_TILES], F32)
         load_copy = keep.tile([P, B_TILES, K], BF16)
         gen_copy = keep.tile([P, B_TILES, K], BF16)
+        products = keep.tile([P, B_TILES, NB], F32)
         for bt in range(B_TILES):
-            nc.scalar.activation(
-                out=load_copy[:, bt, :], in_=loads[:, bt, :], func=COPY, accum_out=load_sum[:, bt : bt + 1]
-            )
+            one = slice(bt, bt + 1)
+            nc.scalar.activation(out=load_copy[:, bt, :], in_=loads[:, bt, :], func=COPY, accum_out=load_sum[:, one])
             nc.vector.tensor_scalar(
                 out=gen_copy[:, bt, :],
                 in0=gens[:, bt, :],
@@ -104,14 +108,8 @@ def tile_kktloss_pc_s_kernel(
                 scalar2=None,
                 op0=MULT,
                 op1=ADD,
-                accum_out=gen_sum[:, bt : bt + 1],
+                accum_out=gen_sum[:, one],
             )
-        net_load = keep.tile([P, B_TILES], F32)
-        nc.vector.tensor_sub(out=net_load[:], in0=load_sum[:], in1=gen_sum[:])
-
-        power = keep.tile([P, B_TILES], F32)
-        products = keep.tile([P, B_TILES, NB], F32)
-        for bt in range(B_TILES):
             acc = psum.tile([P, NB], F32, name="acc%d" % bt)
             for w in range(WEIGHTS):
                 for g in range(PASSES):
@@ -131,10 +129,17 @@ def tile_kktloss_pc_s_kernel(
                 in1=volt[:, bt, 0:NB],
                 op0=MULT,
                 op1=MULT,
-                accum_out=power[:, bt : bt + 1],
+                accum_out=power[:, one],
+            )
+            nc.vector.scalar_tensor_tensor(
+                out=result_cols[:, one],
+                in0=power[:, one],
+                scalar=gen_sum[:, one],
+                in1=load_sum[:, one],
+                op0=SUBTRACT,
+                op1=ADD,
             )
 
-        nc.vector.tensor_add(out=result_cols[:, 0:B_TILES], in0=power[:], in1=net_load[:])
         result_rows_ps = psum.tile([P, P], F32)
         nc.tensor.transpose(result_rows_ps[:], result_cols[:], ident[:])
         result_rows = keep.tile([P, P], F32)

@@ -46,8 +46,8 @@ def tile_kktloss_pc_s_kernel(
         gens = keep.tile([P, B_TILES, K], BF16)
         w_words = keep.tile([P, WEIGHTS, PASSES, 2 * NB], U8, align_bytes=64)
         w_scales = keep.tile([P, WEIGHTS, PASSES, NB], U8, align_bytes=64)
-        v_codes = keep.tile([P, B_TILES, PASSES * P], U32, align_bytes=64)
-        v_scales = keep.tile([P, B_TILES, PASSES * P], U8, align_bytes=64)
+        v_codes = keep.tile([P, B_TILES, PASSES, P], U32, align_bytes=64)
+        v_scales = keep.tile([P, B_TILES, PASSES, P], U8, align_bytes=64)
         ident = keep.tile([P, P], F32)
         result_cols = keep.tile([P, P], F32)
 
@@ -60,37 +60,65 @@ def tile_kktloss_pc_s_kernel(
             for r in range(PACK):
                 nc.sync.dma_start(out=w_scales[r:P:32, w, :, :].bitcast(I32), in_=by_row[r])
 
-        for bt in range(B_TILES):
+        def load_loads_and_gens(bt):
+            nc.sync.dma_start(out=loads[:, bt, :], in_=PQ_Loads[bt * P : (bt + 1) * P, :])
+            nc.sync.dma_start(out=gens[:, bt, :], in_=PQ_Gens[bt * P : (bt + 1) * P, :])
+
+        def load_volt(bt):
             nc.sync.dma_start(out=volt[:, bt, :], in_=Volt[bt * P : (bt + 1) * P, :])
-        load_scale_rows(0)
-        for w in range(WEIGHTS):
+
+        def load_words(w):
             nc.sync.dma_start(
                 out=w_words[:, w, :, :].bitcast(I32),
                 in_=weight_words[w].bitcast(I32).rearrange("g p n -> p g n"),
             )
+
+        load_volt(0)
+        load_scale_rows(0)
+        load_words(0)
+        load_volt(1)
+        load_words(1)
         load_scale_rows(1)
-        for bt in range(B_TILES):
-            nc.gpsimd.dma_start(out=loads[:, bt, :], in_=PQ_Loads[bt * P : (bt + 1) * P, :])
-            nc.gpsimd.dma_start(out=gens[:, bt, :], in_=PQ_Gens[bt * P : (bt + 1) * P, :])
+        load_loads_and_gens(0)
+        load_loads_and_gens(1)
 
         for bt in range(B_TILES):
             volt_words = volt[:, bt, :].bitcast(F32)
-            flipped = psum.tile([P, PASSES, 2, P], F32, name="flipped%d" % bt)
+            grouped = keep.tile([P, PASSES, P, PACK], BF16, align_bytes=64, name="grouped%d" % bt)
             for g in range(PASSES):
+                flipped = psum.tile([P, 2, P], F32, name="flipped%d%d" % (bt, g))
                 for u in range(2):
                     first = g * WORDS_PER_PASS + u
                     nc.tensor.transpose(
-                        flipped[:, g, u, :],
+                        flipped[:, u, :],
                         volt_words[:, first : (g + 1) * WORDS_PER_PASS : 2],
                         ident[:],
                     )
-            grouped = keep.tile([P, PASSES, P, PACK], BF16, align_bytes=64, name="grouped%d" % bt)
-            nc.scalar.copy(out=grouped[:].bitcast(F32), in_=flipped[:].rearrange("p g u b -> p g b u"))
-            nc.vector.quantize_mx(
-                out=v_codes[:, bt, :].bitcast(FP8X4),
-                scales=v_scales[:, bt, :],
-                in_=grouped[:].rearrange("p g b t -> p (g b t)"),
-            )
+                side_by_side = flipped[:].rearrange("p u b -> p b u")
+                if g == 0:
+                    nc.vector.tensor_copy(out=grouped[:, g, :, :].bitcast(F32), in_=side_by_side)
+                else:
+                    nc.scalar.copy(out=grouped[:, g, :, :].bitcast(F32), in_=side_by_side)
+            for g in range(PASSES):
+                nc.vector.quantize_mx(
+                    out=v_codes[:, bt, g, :].bitcast(FP8X4),
+                    scales=v_scales[:, bt, g, :],
+                    in_=grouped[:, g, :, :].rearrange("p b t -> p (b t)"),
+                )
+
+        acc = [psum.tile([P, NB], F32, name="acc%d" % bt) for bt in range(B_TILES)]
+        for bt in range(B_TILES):
+            for w in range(WEIGHTS):
+                for g in range(PASSES):
+                    nc.tensor.matmul_mx(
+                        out=acc[bt][:],
+                        lhsT=v_codes[:, bt, g, :].bitcast(FP8X4),
+                        lhsT_scale=v_scales[:, bt, g, :],
+                        rhs=w_words[:, w, g, :].bitcast(FP4X4),
+                        rhs_scale=w_scales[:, w, g, :],
+                        start=(w == 0 and g == 0),
+                        stop=(w == WEIGHTS - 1 and g == PASSES - 1),
+                    )
 
         load_sum = keep.tile([P, B_TILES], F32)
         gen_sum = keep.tile([P, B_TILES], F32)
@@ -110,21 +138,9 @@ def tile_kktloss_pc_s_kernel(
                 op1=ADD,
                 accum_out=gen_sum[:, one],
             )
-            acc = psum.tile([P, NB], F32, name="acc%d" % bt)
-            for w in range(WEIGHTS):
-                for g in range(PASSES):
-                    nc.tensor.matmul_mx(
-                        out=acc[:],
-                        lhsT=v_codes[:, bt, g * P : (g + 1) * P].bitcast(FP8X4),
-                        lhsT_scale=v_scales[:, bt, g * P : (g + 1) * P],
-                        rhs=w_words[:, w, g, :].bitcast(FP4X4),
-                        rhs_scale=w_scales[:, w, g, :],
-                        start=(w == 0 and g == 0),
-                        stop=(w == WEIGHTS - 1 and g == PASSES - 1),
-                    )
             nc.vector.scalar_tensor_tensor(
                 out=products[:, bt, :],
-                in0=acc[:],
+                in0=acc[bt][:],
                 scalar=1.0,
                 in1=volt[:, bt, 0:NB],
                 op0=MULT,

@@ -25,6 +25,7 @@ PASSES = K // K_PASS
 B_TILES = B // P
 WEIGHTS = 2
 WORDS_PER_PASS = K_PASS // 2
+WARM_UP = (6, 2)
 
 FLOPS = 2 * B * K * NB * WEIGHTS
 
@@ -50,6 +51,14 @@ def tile_kktloss_pc_s_kernel(
         v_scales = keep.tile([P, B_TILES, PASSES, P], U8, align_bytes=64)
         ident = keep.tile([P, P], F32)
         result_cols = keep.tile([P, P], F32)
+
+        zeros = keep.tile([P, P], F32)
+        nc.vector.memset(zeros[:], 0.0)
+        unread = psum.tile([P, P], F32)
+
+        def warm_up(count):
+            for i in range(count):
+                nc.tensor.matmul(out=unread[:], lhsT=zeros[:], rhs=zeros[:], start=True, stop=True)
 
         nc.vector.memset(w_scales[:].bitcast(I32), 0)
         nc.vector.memset(result_cols[:], 0.0)
@@ -83,6 +92,7 @@ def tile_kktloss_pc_s_kernel(
         load_loads_and_gens(1)
 
         for bt in range(B_TILES):
+            warm_up(WARM_UP[bt])
             volt_words = volt[:, bt, :].bitcast(F32)
             grouped = keep.tile([P, PASSES, P, PACK], BF16, align_bytes=64, name="grouped%d" % bt)
             for g in range(PASSES):

@@ -69,10 +69,6 @@ def tile_kktloss_pc_s_kernel(
             for r in range(PACK):
                 nc.sync.dma_start(out=w_scales[r:P:32, w, :, :].bitcast(I32), in_=by_row[r])
 
-        def load_loads_and_gens(bt):
-            nc.sync.dma_start(out=loads[:, bt, :], in_=PQ_Loads[bt * P : (bt + 1) * P, :])
-            nc.sync.dma_start(out=gens[:, bt, :], in_=PQ_Gens[bt * P : (bt + 1) * P, :])
-
         def load_volt(bt):
             nc.sync.dma_start(out=volt[:, bt, :], in_=Volt[bt * P : (bt + 1) * P, :])
 
@@ -88,8 +84,10 @@ def tile_kktloss_pc_s_kernel(
         load_volt(1)
         load_words(1)
         load_scale_rows(1)
-        load_loads_and_gens(0)
-        load_loads_and_gens(1)
+        for bt in range(B_TILES):
+            nc.sync.dma_start(out=gens[:, bt, :], in_=PQ_Gens[bt * P : (bt + 1) * P, :])
+        for bt in range(B_TILES):
+            nc.gpsimd.dma_start(out=loads[:, bt, :], in_=PQ_Loads[bt * P : (bt + 1) * P, :])
 
         for bt in range(B_TILES):
             warm_up(WARM_UP[bt])
@@ -139,15 +137,6 @@ def tile_kktloss_pc_s_kernel(
         for bt in range(B_TILES):
             one = slice(bt, bt + 1)
             nc.scalar.activation(out=load_copy[:, bt, :], in_=loads[:, bt, :], func=COPY, accum_out=load_sum[:, one])
-            nc.vector.tensor_scalar(
-                out=gen_copy[:, bt, :],
-                in0=gens[:, bt, :],
-                scalar1=1.0,
-                scalar2=None,
-                op0=MULT,
-                op1=ADD,
-                accum_out=gen_sum[:, one],
-            )
             nc.vector.scalar_tensor_tensor(
                 out=products[:, bt, :],
                 in0=acc[bt][:],
@@ -156,6 +145,15 @@ def tile_kktloss_pc_s_kernel(
                 op0=MULT,
                 op1=MULT,
                 accum_out=power[:, one],
+            )
+            nc.vector.tensor_scalar(
+                out=gen_copy[:, bt, :],
+                in0=gens[:, bt, :],
+                scalar1=1.0,
+                scalar2=None,
+                op0=MULT,
+                op1=ADD,
+                accum_out=gen_sum[:, one],
             )
             nc.vector.scalar_tensor_tensor(
                 out=result_cols[:, one],

@@ -12,7 +12,6 @@ FP8X4 = mybir.dt.float8_e4m3fn_x4
 FP4X4 = mybir.dt.float4_e2m1fn_x4
 MULT = mybir.AluOpType.mult
 ADD = mybir.AluOpType.add
-SUBTRACT = mybir.AluOpType.subtract
 COPY = mybir.ActivationFunctionType.Copy
 
 P = 128
@@ -25,7 +24,7 @@ PASSES = K // K_PASS
 B_TILES = B // P
 WEIGHTS = 2
 WORDS_PER_PASS = K_PASS // 2
-WARM_UP = (6, 2)
+WARM_UP = 6
 
 FLOPS = 2 * B * K * NB * WEIGHTS
 
@@ -50,24 +49,29 @@ def tile_kktloss_pc_s_kernel(
         v_codes = keep.tile([P, B_TILES, PASSES, P], U32, align_bytes=64)
         v_scales = keep.tile([P, B_TILES, PASSES, P], U8, align_bytes=64)
         ident = keep.tile([P, P], F32)
-        result_cols = keep.tile([P, P], F32)
+        power_cols = keep.tile([P, P], F32)
+        net_load_cols = keep.tile([P, P], F32)
 
         zeros = keep.tile([P, P], F32)
         nc.vector.memset(zeros[:], 0.0)
         unread = psum.tile([P, P], F32)
 
-        def warm_up(count):
-            for i in range(count):
-                nc.tensor.matmul(out=unread[:], lhsT=zeros[:], rhs=zeros[:], start=True, stop=True)
+        for i in range(WARM_UP):
+            nc.tensor.matmul(out=unread[:], lhsT=zeros[:], rhs=zeros[:], start=True, stop=True)
 
         nc.vector.memset(w_scales[:].bitcast(I32), 0)
-        nc.vector.memset(result_cols[:], 0.0)
+        nc.vector.memset(power_cols[:], 0.0)
+        nc.gpsimd.memset(net_load_cols[:], 0.0)
         make_identity(nc, ident[:])
 
         def load_scale_rows(w):
             by_row = weight_scales[w].bitcast(I32).rearrange("g (q r) n -> r q g n", r=PACK)
             for r in range(PACK):
                 nc.sync.dma_start(out=w_scales[r:P:32, w, :, :].bitcast(I32), in_=by_row[r])
+
+        def load_loads_and_gens(bt):
+            nc.sync.dma_start(out=loads[:, bt, :], in_=PQ_Loads[bt * P : (bt + 1) * P, :])
+            nc.sync.dma_start(out=gens[:, bt, :], in_=PQ_Gens[bt * P : (bt + 1) * P, :])
 
         def load_volt(bt):
             nc.sync.dma_start(out=volt[:, bt, :], in_=Volt[bt * P : (bt + 1) * P, :])
@@ -84,13 +88,10 @@ def tile_kktloss_pc_s_kernel(
         load_volt(1)
         load_words(1)
         load_scale_rows(1)
-        for bt in range(B_TILES):
-            nc.sync.dma_start(out=gens[:, bt, :], in_=PQ_Gens[bt * P : (bt + 1) * P, :])
-        for bt in range(B_TILES):
-            nc.gpsimd.dma_start(out=loads[:, bt, :], in_=PQ_Loads[bt * P : (bt + 1) * P, :])
+        load_loads_and_gens(0)
+        load_loads_and_gens(1)
 
         for bt in range(B_TILES):
-            warm_up(WARM_UP[bt])
             volt_words = volt[:, bt, :].bitcast(F32)
             grouped = keep.tile([P, PASSES, P, PACK], BF16, align_bytes=64, name="grouped%d" % bt)
             for g in range(PASSES):
@@ -130,22 +131,12 @@ def tile_kktloss_pc_s_kernel(
 
         load_sum = keep.tile([P, B_TILES], F32)
         gen_sum = keep.tile([P, B_TILES], F32)
-        power = keep.tile([P, B_TILES], F32)
         load_copy = keep.tile([P, B_TILES, K], BF16)
         gen_copy = keep.tile([P, B_TILES, K], BF16)
         products = keep.tile([P, B_TILES, NB], F32)
         for bt in range(B_TILES):
             one = slice(bt, bt + 1)
             nc.scalar.activation(out=load_copy[:, bt, :], in_=loads[:, bt, :], func=COPY, accum_out=load_sum[:, one])
-            nc.vector.scalar_tensor_tensor(
-                out=products[:, bt, :],
-                in0=acc[bt][:],
-                scalar=1.0,
-                in1=volt[:, bt, 0:NB],
-                op0=MULT,
-                op1=MULT,
-                accum_out=power[:, one],
-            )
             nc.vector.tensor_scalar(
                 out=gen_copy[:, bt, :],
                 in0=gens[:, bt, :],
@@ -156,16 +147,23 @@ def tile_kktloss_pc_s_kernel(
                 accum_out=gen_sum[:, one],
             )
             nc.vector.scalar_tensor_tensor(
-                out=result_cols[:, one],
-                in0=power[:, one],
-                scalar=gen_sum[:, one],
-                in1=load_sum[:, one],
-                op0=SUBTRACT,
-                op1=ADD,
+                out=products[:, bt, :],
+                in0=acc[bt][:],
+                scalar=1.0,
+                in1=volt[:, bt, 0:NB],
+                op0=MULT,
+                op1=MULT,
+                accum_out=power_cols[:, one],
             )
+        nc.gpsimd.tensor_sub(out=net_load_cols[:, 0:B_TILES], in0=load_sum[:], in1=gen_sum[:])
 
         result_rows_ps = psum.tile([P, P], F32)
-        nc.tensor.transpose(result_rows_ps[:], result_cols[:], ident[:])
+        nc.tensor.matmul(
+            out=result_rows_ps[:], lhsT=net_load_cols[:], rhs=ident[:], is_transpose=True, start=True, stop=False
+        )
+        nc.tensor.matmul(
+            out=result_rows_ps[:], lhsT=power_cols[:], rhs=ident[:], is_transpose=True, start=False, stop=True
+        )
         result_rows = keep.tile([P, P], F32)
         nc.vector.tensor_copy(out=result_rows[0:B_TILES, :], in_=result_rows_ps[0:B_TILES, :])
         nc.sync.dma_start(out=out.rearrange("(t p) -> t p", p=P), in_=result_rows[0:B_TILES, :])

@@ -24,7 +24,7 @@ PASSES = K // K_PASS
 B_TILES = B // P
 WEIGHTS = 2
 WORDS_PER_PASS = K_PASS // 2
-WARM_UP = 6
+WARM_UP = (6, 2)
 
 FLOPS = 2 * B * K * NB * WEIGHTS
 
@@ -56,8 +56,10 @@ def tile_kktloss_pc_s_kernel(
         nc.vector.memset(zeros[:], 0.0)
         unread = psum.tile([P, P], F32)
 
-        for i in range(WARM_UP):
-            nc.tensor.matmul(out=unread[:], lhsT=zeros[:], rhs=zeros[:], start=True, stop=True)
+
+        def warm_up(count):
+            for i in range(count):
+                nc.tensor.matmul(out=unread[:], lhsT=zeros[:], rhs=zeros[:], start=True, stop=True)
 
         nc.vector.memset(w_scales[:].bitcast(I32), 0)
         nc.vector.memset(power_cols[:], 0.0)
@@ -92,6 +94,7 @@ def tile_kktloss_pc_s_kernel(
         load_loads_and_gens(1)
 
         for bt in range(B_TILES):
+            warm_up(WARM_UP[bt])
             volt_words = volt[:, bt, :].bitcast(F32)
             grouped = keep.tile([P, PASSES, P, PACK], BF16, align_bytes=64, name="grouped%d" % bt)
             for g in range(PASSES):

@@ -22,9 +22,10 @@ PACK = 4
 K_PASS = P * PACK
 PASSES = K // K_PASS
 B_TILES = B // P
+BLOCK = 32
 WEIGHTS = 2
 WORDS_PER_PASS = K_PASS // 2
-WARM_UP = (6, 2)
+WARM_UP = (3, 0)
 
 FLOPS = 2 * B * K * NB * WEIGHTS
 
@@ -50,21 +51,22 @@ def tile_kktloss_pc_s_kernel(
         v_scales = keep.tile([P, B_TILES, PASSES, P], U8, align_bytes=64)
         ident = keep.tile([P, P], F32)
         power_cols = keep.tile([P, P], F32)
-        net_load_cols = keep.tile([P, P], F32)
+        load_cols = keep.tile([P, P], F32)
+        minus_gen_cols = keep.tile([P, P], F32)
 
         zeros = keep.tile([P, P], F32)
         nc.vector.memset(zeros[:], 0.0)
         unread = psum.tile([P, P], F32)
 
-
         def warm_up(count):
             for i in range(count):
                 nc.tensor.matmul(out=unread[:], lhsT=zeros[:], rhs=zeros[:], start=True, stop=True)
 
-        nc.vector.memset(w_scales[:].bitcast(I32), 0)
-        nc.vector.memset(power_cols[:], 0.0)
-        nc.gpsimd.memset(net_load_cols[:], 0.0)
+        nc.gpsimd.memset(w_scales[:].bitcast(F32), 0.0)
         make_identity(nc, ident[:])
+        nc.gpsimd.memset(minus_gen_cols[:], 0.0)
+        nc.gpsimd.memset(load_cols[:], 0.0)
+        nc.gpsimd.memset(power_cols[:], 0.0)
 
         def load_scale_rows(w):
             by_row = weight_scales[w].bitcast(I32).rearrange("g (q r) n -> r q g n", r=PACK)
@@ -86,8 +88,8 @@ def tile_kktloss_pc_s_kernel(
 
         load_volt(0)
         load_scale_rows(0)
-        load_words(0)
         load_volt(1)
+        load_words(0)
         load_words(1)
         load_scale_rows(1)
         load_loads_and_gens(0)
@@ -107,10 +109,7 @@ def tile_kktloss_pc_s_kernel(
                         ident[:],
                     )
                 side_by_side = flipped[:].rearrange("p u b -> p b u")
-                if g == 0:
-                    nc.vector.tensor_copy(out=grouped[:, g, :, :].bitcast(F32), in_=side_by_side)
-                else:
-                    nc.scalar.copy(out=grouped[:, g, :, :].bitcast(F32), in_=side_by_side)
+                nc.scalar.copy(out=grouped[:, g, :, :].bitcast(F32), in_=side_by_side)
             for g in range(PASSES):
                 nc.vector.quantize_mx(
                     out=v_codes[:, bt, g, :].bitcast(FP8X4),
@@ -120,34 +119,32 @@ def tile_kktloss_pc_s_kernel(
 
         acc = [psum.tile([P, NB], F32, name="acc%d" % bt) for bt in range(B_TILES)]
         for bt in range(B_TILES):
-            for w in range(WEIGHTS):
-                for g in range(PASSES):
+            for g in range(PASSES):
+                for w in range(WEIGHTS):
                     nc.tensor.matmul_mx(
                         out=acc[bt][:],
                         lhsT=v_codes[:, bt, g, :].bitcast(FP8X4),
                         lhsT_scale=v_scales[:, bt, g, :],
                         rhs=w_words[:, w, g, :].bitcast(FP4X4),
                         rhs_scale=w_scales[:, w, g, :],
-                        start=(w == 0 and g == 0),
-                        stop=(w == WEIGHTS - 1 and g == PASSES - 1),
+                        start=(g == 0 and w == 0),
+                        stop=(g == PASSES - 1 and w == WEIGHTS - 1),
                     )
 
-        load_sum = keep.tile([P, B_TILES], F32)
-        gen_sum = keep.tile([P, B_TILES], F32)
         load_copy = keep.tile([P, B_TILES, K], BF16)
         gen_copy = keep.tile([P, B_TILES, K], BF16)
         products = keep.tile([P, B_TILES, NB], F32)
         for bt in range(B_TILES):
             one = slice(bt, bt + 1)
-            nc.scalar.activation(out=load_copy[:, bt, :], in_=loads[:, bt, :], func=COPY, accum_out=load_sum[:, one])
+            nc.scalar.activation(out=load_copy[:, bt, :], in_=loads[:, bt, :], func=COPY, accum_out=load_cols[:, one])
             nc.vector.tensor_scalar(
                 out=gen_copy[:, bt, :],
                 in0=gens[:, bt, :],
-                scalar1=1.0,
+                scalar1=-1.0,
                 scalar2=None,
                 op0=MULT,
                 op1=ADD,
-                accum_out=gen_sum[:, one],
+                accum_out=minus_gen_cols[:, one],
             )
             nc.vector.scalar_tensor_tensor(
                 out=products[:, bt, :],
@@ -158,15 +155,14 @@ def tile_kktloss_pc_s_kernel(
                 op1=MULT,
                 accum_out=power_cols[:, one],
             )
-        nc.gpsimd.tensor_sub(out=net_load_cols[:, 0:B_TILES], in0=load_sum[:], in1=gen_sum[:])
 
         result_rows_ps = psum.tile([P, P], F32)
-        nc.tensor.matmul(
-            out=result_rows_ps[:], lhsT=net_load_cols[:], rhs=ident[:], is_transpose=True, start=True, stop=False
-        )
-        nc.tensor.matmul(
-            out=result_rows_ps[:], lhsT=power_cols[:], rhs=ident[:], is_transpose=True, start=False, stop=True
-        )
+        terms = [minus_gen_cols, load_cols, power_cols]
+        for i, term in enumerate(terms):
+            nc.tensor.matmul(
+                out=result_rows_ps[:], lhsT=term[:], rhs=ident[:], is_transpose=True,
+                start=(i == 0), stop=(i == len(terms) - 1),
+            )
         result_rows = keep.tile([P, P], F32)
         nc.vector.tensor_copy(out=result_rows[0:B_TILES, :], in_=result_rows_ps[0:B_TILES, :])
         nc.sync.dma_start(out=out.rearrange("(t p) -> t p", p=P), in_=result_rows[0:B_TILES, :])

@@ -25,7 +25,7 @@ B_TILES = B // P
 BLOCK = 32
 WEIGHTS = 2
 WORDS_PER_PASS = K_PASS // 2
-WARM_UP = (3, 0)
+WARM_UP = (6, 2)
 
 FLOPS = 2 * B * K * NB * WEIGHTS
 

@@ -25,7 +25,8 @@ B_TILES = B // P
 BLOCK = 32
 WEIGHTS = 2
 WORDS_PER_PASS = K_PASS // 2
-WARM_UP = (6, 2)
+WARM_UP_AHEAD = 4
+WARM_UP_BETWEEN = 2
 
 FLOPS = 2 * B * K * NB * WEIGHTS
 
@@ -95,8 +96,8 @@ def tile_kktloss_pc_s_kernel(
         load_loads_and_gens(0)
         load_loads_and_gens(1)
 
+        warm_up(WARM_UP_AHEAD)
         for bt in range(B_TILES):
-            warm_up(WARM_UP[bt])
             volt_words = volt[:, bt, :].bitcast(F32)
             grouped = keep.tile([P, PASSES, P, PACK], BF16, align_bytes=64, name="grouped%d" % bt)
             for g in range(PASSES):
@@ -116,6 +117,8 @@ def tile_kktloss_pc_s_kernel(
                     scales=v_scales[:, bt, g, :],
                     in_=grouped[:, g, :, :].rearrange("p b t -> p (b t)"),
                 )
+
+        warm_up(WARM_UP_BETWEEN)
 
         acc = [psum.tile([P, NB], F32, name="acc%d" % bt) for bt in range(B_TILES)]
         for bt in range(B_TILES):
@@ -137,15 +140,6 @@ def tile_kktloss_pc_s_kernel(
         for bt in range(B_TILES):
             one = slice(bt, bt + 1)
             nc.scalar.activation(out=load_copy[:, bt, :], in_=loads[:, bt, :], func=COPY, accum_out=load_cols[:, one])
-            nc.vector.tensor_scalar(
-                out=gen_copy[:, bt, :],
-                in0=gens[:, bt, :],
-                scalar1=-1.0,
-                scalar2=None,
-                op0=MULT,
-                op1=ADD,
-                accum_out=minus_gen_cols[:, one],
-            )
             nc.vector.scalar_tensor_tensor(
                 out=products[:, bt, :],
                 in0=acc[bt][:],
@@ -155,9 +149,18 @@ def tile_kktloss_pc_s_kernel(
                 op1=MULT,
                 accum_out=power_cols[:, one],
             )
+            nc.vector.tensor_scalar(
+                out=gen_copy[:, bt, :],
+                in0=gens[:, bt, :],
+                scalar1=-1.0,
+                scalar2=None,
+                op0=MULT,
+                op1=ADD,
+                accum_out=minus_gen_cols[:, one],
+            )
 
         result_rows_ps = psum.tile([P, P], F32)
-        terms = [minus_gen_cols, load_cols, power_cols]
+        terms = [power_cols, load_cols, minus_gen_cols]
         for i, term in enumerate(terms):
             nc.tensor.matmul(
                 out=result_rows_ps[:], lhsT=term[:], rhs=ident[:], is_transpose=True,

@@ -140,15 +140,6 @@ def tile_kktloss_pc_s_kernel(
         for bt in range(B_TILES):
             one = slice(bt, bt + 1)
             nc.scalar.activation(out=load_copy[:, bt, :], in_=loads[:, bt, :], func=COPY, accum_out=load_cols[:, one])
-            nc.vector.scalar_tensor_tensor(
-                out=products[:, bt, :],
-                in0=acc[bt][:],
-                scalar=1.0,
-                in1=volt[:, bt, 0:NB],
-                op0=MULT,
-                op1=MULT,
-                accum_out=power_cols[:, one],
-            )
             nc.vector.tensor_scalar(
                 out=gen_copy[:, bt, :],
                 in0=gens[:, bt, :],
@@ -158,9 +149,18 @@ def tile_kktloss_pc_s_kernel(
                 op1=ADD,
                 accum_out=minus_gen_cols[:, one],
             )
+            nc.vector.scalar_tensor_tensor(
+                out=products[:, bt, :],
+                in0=acc[bt][:],
+                scalar=1.0,
+                in1=volt[:, bt, 0:NB],
+                op0=MULT,
+                op1=MULT,
+                accum_out=power_cols[:, one],
+            )
 
         result_rows_ps = psum.tile([P, P], F32)
-        terms = [power_cols, load_cols, minus_gen_cols]
+        terms = [minus_gen_cols, load_cols, power_cols]
         for i, term in enumerate(terms):
             nc.tensor.matmul(
                 out=result_rows_ps[:], lhsT=term[:], rhs=ident[:], is_transpose=True,

@@ -122,16 +122,16 @@ def tile_kktloss_pc_s_kernel(
 
         acc = [psum.tile([P, NB], F32, name="acc%d" % bt) for bt in range(B_TILES)]
         for bt in range(B_TILES):
-            for g in range(PASSES):
-                for w in range(WEIGHTS):
+            for w in range(WEIGHTS):
+                for g in range(PASSES):
                     nc.tensor.matmul_mx(
                         out=acc[bt][:],
                         lhsT=v_codes[:, bt, g, :].bitcast(FP8X4),
                         lhsT_scale=v_scales[:, bt, g, :],
                         rhs=w_words[:, w, g, :].bitcast(FP4X4),
                         rhs_scale=w_scales[:, w, g, :],
-                        start=(g == 0 and w == 0),
-                        stop=(g == PASSES - 1 and w == WEIGHTS - 1),
+                        start=(w == 0 and g == 0),
+                        stop=(w == WEIGHTS - 1 and g == PASSES - 1),
                     )
 
         load_copy = keep.tile([P, B_TILES, K], BF16)

@@ -74,10 +74,6 @@ def tile_kktloss_pc_s_kernel(
             for r in range(PACK):
                 nc.sync.dma_start(out=w_scales[r:P:32, w, :, :].bitcast(I32), in_=by_row[r])
 
-        def load_loads_and_gens(bt):
-            nc.sync.dma_start(out=loads[:, bt, :], in_=PQ_Loads[bt * P : (bt + 1) * P, :])
-            nc.sync.dma_start(out=gens[:, bt, :], in_=PQ_Gens[bt * P : (bt + 1) * P, :])
-
         def load_volt(bt):
             nc.sync.dma_start(out=volt[:, bt, :], in_=Volt[bt * P : (bt + 1) * P, :])
 
@@ -93,8 +89,10 @@ def tile_kktloss_pc_s_kernel(
         load_words(0)
         load_words(1)
         load_scale_rows(1)
-        load_loads_and_gens(0)
-        load_loads_and_gens(1)
+        nc.sync.dma_start(out=gens[:, 0, :], in_=PQ_Gens[0:P, :])
+        nc.sync.dma_start(out=loads[:, 0, :], in_=PQ_Loads[0:P, :])
+        nc.sync.dma_start(out=loads[:, 1, :], in_=PQ_Loads[P : 2 * P, :])
+        nc.sync.dma_start(out=gens[:, 1, :], in_=PQ_Gens[P : 2 * P, :])
 
         warm_up(WARM_UP_AHEAD)
         for bt in range(B_TILES):

@@ -43,13 +43,14 @@ def tile_kktloss_pc_s_kernel(
         psum = stack.enter_context(tc.psum_pool(name="psum", bufs=1))
         stack.enter_context(tc.manual_schedule())
 
-        volt = keep.tile([P, B_TILES, K], BF16)
-        loads = keep.tile([P, B_TILES, K], BF16)
-        gens = keep.tile([P, B_TILES, K], BF16)
-        w_words = keep.tile([P, WEIGHTS, PASSES, 2 * NB], U8, align_bytes=64)
-        w_scales = keep.tile([P, WEIGHTS, PASSES, NB], U8, align_bytes=64)
-        v_codes = keep.tile([P, B_TILES, PASSES, P], U32, align_bytes=64)
-        v_scales = keep.tile([P, B_TILES, PASSES, P], U8, align_bytes=64)
+        volt = [keep.tile([P, K], BF16, name="volt%d" % bt) for bt in range(B_TILES)]
+        loads = [keep.tile([P, K], BF16, name="loads%d" % bt) for bt in range(B_TILES)]
+        gens = [keep.tile([P, K], BF16, name="gens%d" % bt) for bt in range(B_TILES)]
+        w_words = [keep.tile([P, PASSES, 2 * NB], U8, align_bytes=64, name="w_words%d" % w) for w in range(WEIGHTS)]
+        w_scales = [keep.tile([P, PASSES, NB], U8, align_bytes=64, name="w_scales%d" % w) for w in range(WEIGHTS)]
+        steps = [(bt, g) for bt in range(B_TILES) for g in range(PASSES)]
+        v_codes = {(bt, g): keep.tile([P, P], U32, align_bytes=64, name="v_codes%d%d" % (bt, g)) for bt, g in steps}
+        v_scales = {(bt, g): keep.tile([P, P], U8, align_bytes=64, name="v_scales%d%d" % (bt, g)) for bt, g in steps}
         ident = keep.tile([P, P], F32)
         power_cols = keep.tile([P, P], F32)
         load_cols = keep.tile([P, P], F32)
@@ -63,7 +64,8 @@ def tile_kktloss_pc_s_kernel(
             for i in range(count):
                 nc.tensor.matmul(out=unread[:], lhsT=zeros[:], rhs=zeros[:], start=True, stop=True)
 
-        nc.gpsimd.memset(w_scales[:].bitcast(F32), 0.0)
+        for w in range(WEIGHTS):
+            nc.gpsimd.memset(w_scales[w][:].bitcast(F32), 0.0)
         make_identity(nc, ident[:])
         nc.gpsimd.memset(minus_gen_cols[:], 0.0)
         nc.gpsimd.memset(load_cols[:], 0.0)
@@ -72,14 +74,14 @@ def tile_kktloss_pc_s_kernel(
         def load_scale_rows(w):
             by_row = weight_scales[w].bitcast(I32).rearrange("g (q r) n -> r q g n", r=PACK)
             for r in range(PACK):
-                nc.sync.dma_start(out=w_scales[r:P:32, w, :, :].bitcast(I32), in_=by_row[r])
+                nc.sync.dma_start(out=w_scales[w][r:P:32, :, :].bitcast(I32), in_=by_row[r])
 
         def load_volt(bt):
-            nc.sync.dma_start(out=volt[:, bt, :], in_=Volt[bt * P : (bt + 1) * P, :])
+            nc.sync.dma_start(out=volt[bt][:], in_=Volt[bt * P : (bt + 1) * P, :])
 
         def load_words(w):
             nc.sync.dma_start(
-                out=w_words[:, w, :, :].bitcast(I32),
+                out=w_words[w][:].bitcast(I32),
                 in_=weight_words[w].bitcast(I32).rearrange("g p n -> p g n"),
             )
 
@@ -89,15 +91,15 @@ def tile_kktloss_pc_s_kernel(
         load_words(0)
         load_words(1)
         load_scale_rows(1)
-        nc.sync.dma_start(out=gens[:, 0, :], in_=PQ_Gens[0:P, :])
-        nc.sync.dma_start(out=loads[:, 0, :], in_=PQ_Loads[0:P, :])
-        nc.sync.dma_start(out=loads[:, 1, :], in_=PQ_Loads[P : 2 * P, :])
-        nc.sync.dma_start(out=gens[:, 1, :], in_=PQ_Gens[P : 2 * P, :])
+        nc.sync.dma_start(out=gens[0][:], in_=PQ_Gens[0:P, :])
+        nc.sync.dma_start(out=loads[0][:], in_=PQ_Loads[0:P, :])
+        nc.sync.dma_start(out=loads[1][:], in_=PQ_Loads[P : 2 * P, :])
+        nc.sync.dma_start(out=gens[1][:], in_=PQ_Gens[P : 2 * P, :])
 
         warm_up(WARM_UP_AHEAD)
         for bt in range(B_TILES):
-            volt_words = volt[:, bt, :].bitcast(F32)
-            grouped = keep.tile([P, PASSES, P, PACK], BF16, align_bytes=64, name="grouped%d" % bt)
+            volt_words = volt[bt][:].bitcast(F32)
+            grouped = [keep.tile([P, P, PACK], BF16, align_bytes=64, name="grouped%d%d" % (bt, g)) for g in range(PASSES)]
             for g in range(PASSES):
                 flipped = psum.tile([P, 2, P], F32, name="flipped%d%d" % (bt, g))
                 for u in range(2):
@@ -108,12 +110,12 @@ def tile_kktloss_pc_s_kernel(
                         ident[:],
                     )
                 side_by_side = flipped[:].rearrange("p u b -> p b u")
-                nc.scalar.copy(out=grouped[:, g, :, :].bitcast(F32), in_=side_by_side)
+                nc.scalar.copy(out=grouped[g][:].bitcast(F32), in_=side_by_side)
             for g in range(PASSES):
                 nc.vector.quantize_mx(
-                    out=v_codes[:, bt, g, :].bitcast(FP8X4),
-                    scales=v_scales[:, bt, g, :],
-                    in_=grouped[:, g, :, :].rearrange("p b t -> p (b t)"),
+                    out=v_codes[bt, g][:].bitcast(FP8X4),
+                    scales=v_scales[bt, g][:],
+                    in_=grouped[g][:].rearrange("p b t -> p (b t)"),
                 )
 
         warm_up(WARM_UP_BETWEEN)
@@ -124,10 +126,10 @@ def tile_kktloss_pc_s_kernel(
                 for g in range(PASSES):
                     nc.tensor.matmul_mx(
                         out=acc[bt][:],
-                        lhsT=v_codes[:, bt, g, :].bitcast(FP8X4),
-                        lhsT_scale=v_scales[:, bt, g, :],
-                        rhs=w_words[:, w, g, :].bitcast(FP4X4),
-                        rhs_scale=w_scales[:, w, g, :],
+                        lhsT=v_codes[bt, g][:].bitcast(FP8X4),
+                        lhsT_scale=v_scales[bt, g][:],
+                        rhs=w_words[w][:, g, :].bitcast(FP4X4),
+                        rhs_scale=w_scales[w][:, g, :],
                         start=(w == 0 and g == 0),
                         stop=(w == WEIGHTS - 1 and g == PASSES - 1),
                     )
@@ -137,10 +139,10 @@ def tile_kktloss_pc_s_kernel(
         products = keep.tile([P, B_TILES, NB], F32)
         for bt in range(B_TILES):
             one = slice(bt, bt + 1)
-            nc.scalar.activation(out=load_copy[:, bt, :], in_=loads[:, bt, :], func=COPY, accum_out=load_cols[:, one])
+            nc.scalar.activation(out=load_copy[:, bt, :], in_=loads[bt][:], func=COPY, accum_out=load_cols[:, one])
             nc.vector.tensor_scalar(
                 out=gen_copy[:, bt, :],
-                in0=gens[:, bt, :],
+                in0=gens[bt][:],
                 scalar1=-1.0,
                 scalar2=None,
                 op0=MULT,
@@ -151,7 +153,7 @@ def tile_kktloss_pc_s_kernel(
                 out=products[:, bt, :],
                 in0=acc[bt][:],
                 scalar=1.0,
-                in1=volt[:, bt, 0:NB],
+                in1=volt[bt][:, 0:NB],
                 op0=MULT,
                 op1=MULT,
                 accum_out=power_cols[:, one],

from contextlib import ExitStack

import concourse.mybir as mybir
from concourse.masks import make_identity

F32 = mybir.dt.float32
BF16 = mybir.dt.bfloat16
I32 = mybir.dt.int32
U32 = mybir.dt.uint32
U8 = mybir.dt.uint8
FP8X4 = mybir.dt.float8_e4m3fn_x4
FP4X4 = mybir.dt.float4_e2m1fn_x4
MULT = mybir.AluOpType.mult
ADD = mybir.AluOpType.add
COPY = mybir.ActivationFunctionType.Copy

P = 128
B = 256
K = 1024
NB = 512
PACK = 4
K_PASS = P * PACK
PASSES = K // K_PASS
B_TILES = B // P
BLOCK = 32
WEIGHTS = 2
WORDS_PER_PASS = K_PASS // 2
WARM_UP_AHEAD = 4
WARM_UP_BETWEEN = 2

FLOPS = 2 * B * K * NB * WEIGHTS


def tile_kktloss_pc_s_kernel(
    tc, Volt, Y_top_words, Y_top_scales, Yconj_top_words, Yconj_top_scales, PQ_Loads, PQ_Gens, out
):
    nc = tc.nc
    weight_words = [Y_top_words, Yconj_top_words]
    weight_scales = [Y_top_scales, Yconj_top_scales]

    with ExitStack() as stack:
        keep = stack.enter_context(tc.tile_pool(name="keep", bufs=1))
        psum = stack.enter_context(tc.psum_pool(name="psum", bufs=1))
        stack.enter_context(tc.manual_schedule())

        volt = [keep.tile([P, K], BF16, name="volt%d" % bt) for bt in range(B_TILES)]
        loads = [keep.tile([P, K], BF16, name="loads%d" % bt) for bt in range(B_TILES)]
        gens = [keep.tile([P, K], BF16, name="gens%d" % bt) for bt in range(B_TILES)]
        w_words = [keep.tile([P, PASSES, 2 * NB], U8, align_bytes=64, name="w_words%d" % w) for w in range(WEIGHTS)]
        w_scales = [keep.tile([P, PASSES, NB], U8, align_bytes=64, name="w_scales%d" % w) for w in range(WEIGHTS)]
        steps = [(bt, g) for bt in range(B_TILES) for g in range(PASSES)]
        v_codes = {(bt, g): keep.tile([P, P], U32, align_bytes=64, name="v_codes%d%d" % (bt, g)) for bt, g in steps}
        v_scales = {(bt, g): keep.tile([P, P], U8, align_bytes=64, name="v_scales%d%d" % (bt, g)) for bt, g in steps}
        ident = keep.tile([P, P], F32)
        power_cols = keep.tile([P, P], F32)
        load_cols = keep.tile([P, P], F32)
        minus_gen_cols = keep.tile([P, P], F32)

        zeros = keep.tile([P, P], F32)
        nc.vector.memset(zeros[:], 0.0)
        unread = psum.tile([P, P], F32)

        def warm_up(count):
            for i in range(count):
                nc.tensor.matmul(out=unread[:], lhsT=zeros[:], rhs=zeros[:], start=True, stop=True)

        for w in range(WEIGHTS):
            nc.gpsimd.memset(w_scales[w][:].bitcast(F32), 0.0)
        make_identity(nc, ident[:])
        nc.gpsimd.memset(minus_gen_cols[:], 0.0)
        nc.gpsimd.memset(load_cols[:], 0.0)
        nc.gpsimd.memset(power_cols[:], 0.0)

        def load_scale_rows(w):
            by_row = weight_scales[w].bitcast(I32).rearrange("g (q r) n -> r q g n", r=PACK)
            for r in range(PACK):
                nc.sync.dma_start(out=w_scales[w][r:P:32, :, :].bitcast(I32), in_=by_row[r])

        def load_volt(bt):
            nc.sync.dma_start(out=volt[bt][:], in_=Volt[bt * P : (bt + 1) * P, :])

        def load_words(w):
            nc.sync.dma_start(
                out=w_words[w][:].bitcast(I32),
                in_=weight_words[w].bitcast(I32).rearrange("g p n -> p g n"),
            )

        load_volt(0)
        load_scale_rows(0)
        load_volt(1)
        load_words(0)
        load_words(1)
        load_scale_rows(1)
        nc.sync.dma_start(out=gens[0][:], in_=PQ_Gens[0:P, :])
        nc.sync.dma_start(out=loads[0][:], in_=PQ_Loads[0:P, :])
        nc.sync.dma_start(out=loads[1][:], in_=PQ_Loads[P : 2 * P, :])
        nc.sync.dma_start(out=gens[1][:], in_=PQ_Gens[P : 2 * P, :])

        warm_up(WARM_UP_AHEAD)
        for bt in range(B_TILES):
            volt_words = volt[bt][:].bitcast(F32)
            grouped = [keep.tile([P, P, PACK], BF16, align_bytes=64, name="grouped%d%d" % (bt, g)) for g in range(PASSES)]
            for g in range(PASSES):
                flipped = psum.tile([P, 2, P], F32, name="flipped%d%d" % (bt, g))
                for u in range(2):
                    first = g * WORDS_PER_PASS + u
                    nc.tensor.transpose(
                        flipped[:, u, :],
                        volt_words[:, first : (g + 1) * WORDS_PER_PASS : 2],
                        ident[:],
                    )
                side_by_side = flipped[:].rearrange("p u b -> p b u")
                nc.scalar.copy(out=grouped[g][:].bitcast(F32), in_=side_by_side)
            for g in range(PASSES):
                nc.vector.quantize_mx(
                    out=v_codes[bt, g][:].bitcast(FP8X4),
                    scales=v_scales[bt, g][:],
                    in_=grouped[g][:].rearrange("p b t -> p (b t)"),
                )

        warm_up(WARM_UP_BETWEEN)

        acc = [psum.tile([P, NB], F32, name="acc%d" % bt) for bt in range(B_TILES)]
        for bt in range(B_TILES):
            for w in range(WEIGHTS):
                for g in range(PASSES):
                    nc.tensor.matmul_mx(
                        out=acc[bt][:],
                        lhsT=v_codes[bt, g][:].bitcast(FP8X4),
                        lhsT_scale=v_scales[bt, g][:],
                        rhs=w_words[w][:, g, :].bitcast(FP4X4),
                        rhs_scale=w_scales[w][:, g, :],
                        start=(w == 0 and g == 0),
                        stop=(w == WEIGHTS - 1 and g == PASSES - 1),
                    )

        load_copy = keep.tile([P, B_TILES, K], BF16)
        gen_copy = keep.tile([P, B_TILES, K], BF16)
        products = keep.tile([P, B_TILES, NB], F32)
        for bt in range(B_TILES):
            one = slice(bt, bt + 1)
            nc.scalar.activation(out=load_copy[:, bt, :], in_=loads[bt][:], func=COPY, accum_out=load_cols[:, one])
            nc.vector.tensor_scalar(
                out=gen_copy[:, bt, :],
                in0=gens[bt][:],
                scalar1=-1.0,
                scalar2=None,
                op0=MULT,
                op1=ADD,
                accum_out=minus_gen_cols[:, one],
            )
            nc.vector.scalar_tensor_tensor(
                out=products[:, bt, :],
                in0=acc[bt][:],
                scalar=1.0,
                in1=volt[bt][:, 0:NB],
                op0=MULT,
                op1=MULT,
                accum_out=power_cols[:, one],
            )

        result_rows_ps = psum.tile([P, P], F32)
        terms = [minus_gen_cols, load_cols, power_cols]
        for i, term in enumerate(terms):
            nc.tensor.matmul(
                out=result_rows_ps[:], lhsT=term[:], rhs=ident[:], is_transpose=True,
                start=(i == 0), stop=(i == len(terms) - 1),
            )
        result_rows = keep.tile([P, P], F32)
        nc.vector.tensor_copy(out=result_rows[0:B_TILES, :], in_=result_rows_ps[0:B_TILES, :])
        nc.sync.dma_start(out=out.rearrange("(t p) -> t p", p=P), in_=result_rows[0:B_TILES, :])
